import numpy as np
import ml_dtypes


def mxq(x, axis, fmt="e4m3"):
    dtype, down = {"e4m3": (ml_dtypes.float8_e4m3fn, 7), "e5m2": (ml_dtypes.float8_e5m2, 14)}[fmt]
    v = np.moveaxis(np.asarray(x, np.float32).astype(ml_dtypes.bfloat16).astype(np.float64), axis, -1)
    blocks = v.reshape(v.shape[:-1] + (-1, 32))
    amax = np.abs(blocks).max(-1, keepdims=True)
    byte = np.maximum(np.where(amax > 0, np.frexp(amax)[1] - 1 + 127, 0) - down, 1)
    scale = np.exp2(byte - 127.0)
    codes = (blocks / scale).astype(np.float32).astype(dtype).astype(np.float64)
    return np.moveaxis((codes * scale).reshape(v.shape), -1, axis)


WIDE = False


def mx_kscale(k):
    if not WIDE:
        return np.ones(k)
    levels = np.array([10, -10, 5, -5, 0])
    if k % 512:
        return np.exp2(np.random.permutation(np.resize(levels, k // 32))).repeat(32)
    a = np.empty((k // 512, 16))
    for p in range(k // 512):
        a[p, :8] = np.random.permutation(np.resize(levels, 8))
        for g in range(8):
            far = levels[np.abs(levels - a[p, g]) >= 10]
            a[p, g + 8] = far[np.random.randint(len(far))]
    return np.exp2(a.ravel()).repeat(32)


BF16 = ml_dtypes.bfloat16


def bf(x):
    return np.asarray(x, np.float32).astype(BF16)


def f64(x):
    return np.asarray(x).astype(np.float64)


B, S, H, HD = 4, 2048, 4, 128
DIM = H * HD


def draw0():
    s, t = mx_kscale(DIM), mx_kscale(DIM)
    return {"x": bf(np.random.standard_normal((B, S, DIM)) * 2.0 * s),
            "y_norm": bf(np.random.standard_normal((B, S, DIM))),
            "wg_w": bf(np.random.standard_normal((DIM, DIM)) * 0.5 / np.sqrt(DIM) / s[:, None] * t),
            "wo_w": bf(np.random.standard_normal((DIM, DIM)) * 1.5 / np.sqrt(DIM) / t[:, None])}


def core(x, y_norm, wg_w, wo_w):
    g = np.maximum(mxq(f64(x), 2, "e4m3") @ mxq(f64(wg_w), 0, "e4m3"), 0.0)
    h = g * f64(y_norm)
    return mxq(h, 2, "e4m3") @ mxq(f64(wo_w), 0, "e4m3")


def e4m3fn_bytes(y):
    return np.clip(np.asarray(y, np.float64), -448.0, 448.0).astype(np.float32).astype(ml_dtypes.float8_e4m3fn).view(np.uint8)


def e4m3fn_values(b):
    return np.asarray(b, np.uint8).view(ml_dtypes.float8_e4m3fn).astype(np.float64)


def setup_inputs():
    d = draw0()
    x0 = np.asarray(d['x']).astype(np.float64)
    s = (np.max(np.abs(x0), axis=(0, 1), keepdims=True) / 448.0).astype(np.float32)
    out = {}
    for k, v in d.items():
        if k == 'x':
            out['x_bytes'] = e4m3fn_bytes(x0 / s.astype(np.float64))
            out['x_scale'] = s
        else:
            out[k] = v
    return out


def reference(x_bytes, x_scale, y_norm, wg_w, wo_w):
    return core(e4m3fn_values(x_bytes) * x_scale.astype(np.float64), y_norm, wg_w, wo_w)

@@ -1,0 +1,213 @@
+from contextlib import ExitStack
+
+import concourse.mybir as mybir
+from concourse.masks import make_identity
+
+P = 128
+PACK = 4
+DIM = 512
+TOKENS = 4 * 2048
+ROWS = 8
+CHUNK = P * ROWS
+CHUNKS = TOKENS // CHUNK
+PAIR = 2
+UNITS_PER_CHUNK = ROWS // PAIR
+UNITS = CHUNKS * UNITS_PER_CHUNK
+
+FLOPS = 2 * 2 * TOKENS * DIM * DIM
+
+F32 = mybir.dt.float32
+BF16 = mybir.dt.bfloat16
+U32 = mybir.dt.uint32
+U8 = mybir.dt.uint8
+FP8 = mybir.dt.float8_e4m3fn
+FP8X4 = mybir.dt.float8_e4m3fn_x4
+ALU = mybir.AluOpType
+
+
+def tile_multiscaleretention_pb_t_kernel(tc, x_bytes, x_scale, y_norm, wg_w, wo_w, out):
+    nc = tc.nc
+    x_hbm = x_bytes.rearrange("b s k -> (b s) k").rearrange("(c p j) k -> c p j k", p=P, j=ROWS)
+    y_hbm = y_norm.rearrange("b s k -> (b s) k").rearrange("(c p j) k -> c p j k", p=P, j=ROWS)
+    out_hbm = out.rearrange("b s k -> (b s) k").rearrange("(c p j) k -> c p j k", p=P, j=ROWS)
+
+    with ExitStack() as ctx:
+        keep = ctx.enter_context(tc.tile_pool(name="keep", bufs=1))
+        work = ctx.enter_context(tc.tile_pool(name="work", bufs=3))
+        psum = ctx.enter_context(tc.psum_pool(name="psum", bufs=2))
+        ctx.enter_context(tc.manual_schedule())
+
+        x_raw = [keep.tile([P, ROWS, DIM], U8, name=f"x_raw{c}", align_bytes=64) for c in range(CHUNKS)]
+        y_raw = [keep.tile([P, ROWS, DIM], BF16, name=f"y_raw{c}", align_bytes=64) for c in range(CHUNKS)]
+        scale_col = keep.tile([P, PACK], F32, name="scale_col")
+        scale_row = keep.tile([P, PAIR, DIM], F32, name="scale_row", align_bytes=64)
+        ident = keep.tile([P, P], F32, name="ident")
+        wg_raw = keep.tile([P, PACK, DIM], BF16, name="wg_raw", align_bytes=64)
+        wo_raw = keep.tile([P, PACK, DIM], BF16, name="wo_raw", align_bytes=64)
+        wg_grouped = keep.tile([P, DIM * PACK], BF16, name="wg_grouped", align_bytes=64)
+        wo_grouped = keep.tile([P, DIM * PACK], BF16, name="wo_grouped", align_bytes=64)
+        wg_codes = keep.tile([P, DIM], U32, name="wg_codes", align_bytes=64)
+        wo_codes = keep.tile([P, DIM], U32, name="wo_codes", align_bytes=64)
+        wg_scales = keep.tile([P, DIM], U8, name="wg_scales", align_bytes=64)
+        wo_scales = keep.tile([P, DIM], U8, name="wo_scales", align_bytes=64)
+
+        def load_x(c, rows):
+            nc.sync.dma_start(out=x_raw[c][:, rows, :], in_=x_hbm[c][:, rows, :])
+
+        def load_y(c, rows):
+            nc.sync.dma_start(out=y_raw[c][:, rows, :], in_=y_hbm[c][:, rows, :])
+
+        everything = slice(0, ROWS)
+        first = slice(0, PAIR)
+        rest = slice(PAIR, ROWS)
+        nc.sync.dma_start(out=scale_col[:], in_=x_scale.rearrange("a b (p t) -> p (a b t)", t=PACK))
+        load_x(0, first)
+        nc.sync.dma_start(out=wg_raw[:], in_=wg_w.rearrange("(p j) n -> p j n", j=PACK))
+        load_x(0, rest)
+        load_y(0, first)
+        nc.sync.dma_start(out=wo_raw[:], in_=wo_w.rearrange("(p j) n -> p j n", j=PACK))
+        load_y(0, rest)
+        load_x(1, everything)
+        load_y(1, everything)
+
+        make_identity(nc, ident[:])
+        spread = psum.tile([P, PACK, P], F32, name="spread", tag="words", bufs=4)
+        for t in range(PACK):
+            nc.tensor.transpose(spread[:, t, :], scale_col[:, t : t + 1].to_broadcast([P, P]), ident[:])
+        spread_by_k = spread[:].rearrange("p t n -> p n t")
+        nc.vector.tensor_copy(out=scale_row[:, 0, :].rearrange("p (n t) -> p n t", t=PACK), in_=spread_by_k)
+        nc.scalar.copy(out=scale_row[:, 1, :].rearrange("p (n t) -> p n t", t=PACK), in_=spread_by_k)
+
+        x_scaled = {}
+        x_grouped = {}
+        y_grouped = {}
+        x_mx = {}
+        gates = {}
+        h_grouped = {}
+        h_mx = {}
+
+        def rows_of(u):
+            c, i = divmod(u, UNITS_PER_CHUNK)
+            return c, slice(i * PAIR, (i + 1) * PAIR)
+
+        def product(u):
+            c, rows = rows_of(u)
+            x_scaled[u] = work.tile([P, PAIR * DIM], BF16, name=f"x_scaled{u}", tag="x_scaled", align_bytes=64)
+            codes = x_raw[c][:, rows, :].rearrange("p j k -> p (j k)").bitcast(FP8)
+            scales = scale_row[:].rearrange("p j k -> p (j k)")
+            pieces = PAIR if u == 0 else 1
+            width = PAIR * DIM // pieces
+            for i in range(pieces):
+                cols = slice(i * width, (i + 1) * width)
+                nc.vector.tensor_tensor(out=x_scaled[u][:, cols], in0=codes[:, cols], in1=scales[:, cols], op=ALU.mult)
+
+        def transpose_pair(name, words):
+            turned = psum.tile([P, PAIR, 2, P], F32, name=name, tag="words", bufs=4)
+            for j in range(PAIR):
+                for half in range(2):
+                    nc.tensor.transpose(turned[:, j, half, :], words[:, j, half : DIM // 2 : 2], ident[:])
+            return turned
+
+        def group(store, u, name, turned):
+            store[u] = work.tile([P, PAIR, P * PACK], BF16, name=f"{name}{u}", tag=name, align_bytes=64)
+            nc.scalar.copy(
+                out=store[u][:].rearrange("p j n -> p (j n)").bitcast(F32).rearrange("p (j n h) -> p j n h", j=PAIR, h=2),
+                in_=turned[:].rearrange("p j h n -> p j n h"),
+            )
+
+        def turn(u):
+            c, rows = rows_of(u)
+            x_words = x_scaled[u][:].bitcast(F32).rearrange("p (j w) -> p j w", j=PAIR)
+            x_turned = transpose_pair(f"x_turned{u}", x_words)
+            y_words = y_raw[c][:, rows, :].rearrange("p j k -> p (j k)").bitcast(F32).rearrange("p (j w) -> p j w", j=PAIR)
+            y_turned = transpose_pair(f"y_turned{u}", y_words)
+            group(x_grouped, u, "x_grouped", x_turned)
+            group(y_grouped, u, "y_grouped", y_turned)
+
+        def quantize(codes, scales, grouped):
+            nc.vector.quantize_mx(out=codes.bitcast(FP8X4), scales=scales, in_=grouped)
+
+        def quantize_unit(name, u, grouped):
+            codes = work.tile([P, PAIR * P], U32, name=f"{name}_codes{u}", tag=f"{name}_codes", align_bytes=64)
+            scales = work.tile([P, PAIR * P], U8, name=f"{name}_scales{u}", tag=f"{name}_scales", align_bytes=64)
+            quantize(codes[:], scales[:], grouped[:].rearrange("p j n -> p (j n)"))
+            return codes, scales
+
+        def multiply(dst, left, left_cols, right, right_cols):
+            nc.tensor.matmul_mx(
+                out=dst,
+                lhsT=left[0][:, left_cols].bitcast(FP8X4),
+                lhsT_scale=left[1][:, left_cols],
+                rhs=right[0][:, right_cols].bitcast(FP8X4),
+                rhs_scale=right[1][:, right_cols],
+                start=True,
+                stop=True,
+            )
+
+        def gate_matmuls(u):
+            for j in range(PAIR):
+                gates[u, j] = psum.tile([P, PACK, P], F32, name=f"gate{u}_{j}", tag="gate", bufs=2)
+                for t in range(PACK):
+                    multiply(gates[u, j][:, t, :], (wg_codes, wg_scales), slice(t * P, (t + 1) * P), x_mx[u], slice(j * P, (j + 1) * P))
+
+        def gated(u):
+            h_grouped[u] = work.tile([P, PAIR, P * PACK], BF16, name=f"h_grouped{u}", tag="h_grouped", align_bytes=64)
+            for j in range(PAIR):
+                nc.vector.scalar_tensor_tensor(
+                    out=h_grouped[u][:, j, :].rearrange("p (n t) -> p n t", t=PACK),
+                    in0=gates[u, j][:].rearrange("p t n -> p n t"),
+                    scalar=0.0,
+                    in1=y_grouped[u][:, j, :].rearrange("p (n t) -> p n t", t=PACK),
+                    op0=ALU.max,
+                    op1=ALU.mult,
+                )
+
+        def output(u):
+            c, rows = rows_of(u)
+            result = work.tile([P, PAIR, DIM], F32, name=f"result{u}", tag="result", bufs=4)
+            accs = []
+            for j in range(PAIR):
+                acc = psum.tile([P, DIM], F32, name=f"acc{u}_{j}", tag="acc", bufs=2)
+                multiply(acc[:], h_mx[u], slice(j * P, (j + 1) * P), (wo_codes, wo_scales), slice(0, DIM))
+                accs.append(acc)
+            if u < UNITS - 1:
+                for j in range(PAIR):
+                    nc.scalar.copy(out=result[:, j, :], in_=accs[j][:])
+                nc.sync.dma_start(out=out_hbm[c][:, rows, :], in_=result[:])
+            else:
+                nc.scalar.copy(out=result[:, 0, :], in_=accs[0][:])
+                nc.vector.tensor_copy(out=result[:, 1, :], in_=accs[1][:])
+                for j in range(PAIR):
+                    nc.sync.dma_start(out=out_hbm[c][:, rows.start + j, :], in_=result[:, j, :])
+
+        for s in range(-3, UNITS + 1):
+            if s >= 0 and s % UNITS_PER_CHUNK == 0 and s // UNITS_PER_CHUNK + 2 < CHUNKS:
+                load_x(s // UNITS_PER_CHUNK + 2, everything)
+                load_y(s // UNITS_PER_CHUNK + 2, everything)
+            if 0 <= s - 1:
+                output(s - 1)
+            if 0 <= s < UNITS:
+                gated(s)
+            if 0 <= s + 2 < UNITS:
+                turn(s + 2)
+            if s == -1:
+                nc.scalar.copy(
+                    out=wo_grouped[:].rearrange("p (n j) -> p n j", j=PACK),
+                    in_=wo_raw[:].rearrange("p j n -> p n j"),
+                )
+            if 0 <= s + 1 < UNITS:
+                x_mx[s + 1] = quantize_unit("x", s + 1, x_grouped[s + 1])
+                gate_matmuls(s + 1)
+            if s + 3 < UNITS:
+                product(s + 3)
+            if s == -3:
+                nc.vector.tensor_copy(
+                    out=wg_grouped[:].rearrange("p (t m j) -> p t m j", t=PACK, j=PACK),
+                    in_=wg_raw[:].rearrange("p j (m t) -> p t m j", t=PACK),
+                )
+            if s == -2:
+                quantize(wg_codes[:], wg_scales[:], wg_grouped[:])
+            if 0 <= s < UNITS:
+                h_mx[s] = quantize_unit("h", s, h_grouped[s])
+            if s == 0:
+                quantize(wo_codes[:], wo_scales[:], wo_grouped[:])

@@ -78,6 +78,8 @@ def tile_multiscaleretention_pb_t_kernel(tc, x_bytes, x_scale, y_norm, wg_w, wo_
         nc.vector.tensor_copy(out=scale_row[:, 0, :].rearrange("p (n t) -> p n t", t=PACK), in_=spread_by_k)
         nc.scalar.copy(out=scale_row[:, 1, :].rearrange("p (n t) -> p n t", t=PACK), in_=spread_by_k)
 
+        h_ring = [keep.tile([P, PAIR, P * PACK], BF16, name=f"h_ring{i}", align_bytes=64) for i in range(3)]
+        x_wide = {}
         x_scaled = {}
         x_grouped = {}
         y_grouped = {}
@@ -90,22 +92,35 @@ def tile_multiscaleretention_pb_t_kernel(tc, x_bytes, x_scale, y_norm, wg_w, wo_
             c, i = divmod(u, UNITS_PER_CHUNK)
             return c, slice(i * PAIR, (i + 1) * PAIR)
 
+        def helped(u):
+            return u >= 4 and u % 2 == 0
+
+        def widen(u):
+            c, rows = rows_of(u)
+            x_wide[u] = work.tile([P, DIM], BF16, name=f"x_wide{u}", tag="x_wide", align_bytes=64)
+            nc.scalar.copy(out=x_wide[u][:], in_=x_raw[c][:, rows.stop - 1, :].bitcast(FP8))
+
         def product(u):
             c, rows = rows_of(u)
-            x_scaled[u] = work.tile([P, PAIR * DIM], BF16, name=f"x_scaled{u}", tag="x_scaled", align_bytes=64)
+            scaled = work.tile([P, PAIR * DIM], BF16, name=f"x_scaled{u}", tag="x_scaled", align_bytes=64)
             codes = x_raw[c][:, rows, :].rearrange("p j k -> p (j k)").bitcast(FP8)
             scales = scale_row[:].rearrange("p j k -> p (j k)")
-            pieces = PAIR if u == 0 else 1
+            pieces = PAIR if u == 0 or helped(u) else 1
             width = PAIR * DIM // pieces
-            for i in range(pieces):
+            for i in range(1 if helped(u) else pieces):
                 cols = slice(i * width, (i + 1) * width)
-                nc.vector.tensor_tensor(out=x_scaled[u][:, cols], in0=codes[:, cols], in1=scales[:, cols], op=ALU.mult)
+                nc.vector.tensor_tensor(out=scaled[:, cols], in0=codes[:, cols], in1=scales[:, cols], op=ALU.mult)
+            x_scaled[u] = [scaled[:, :DIM], scaled[:, DIM:]]
+
+        def product_gpsimd(u):
+            x_scaled[u][1] = h_ring[(u - 4) % 3][:, 0, :]
+            nc.gpsimd.tensor_tensor(out=x_scaled[u][1], in0=x_wide[u][:], in1=scale_row[:, 1, :], op=ALU.mult)
 
         def transpose_pair(name, words):
             turned = psum.tile([P, PAIR, 2, P], F32, name=name, tag="words", bufs=4)
             for j in range(PAIR):
                 for half in range(2):
-                    nc.tensor.transpose(turned[:, j, half, :], words[:, j, half : DIM // 2 : 2], ident[:])
+                    nc.tensor.transpose(turned[:, j, half, :], words[j][:, half : DIM // 2 : 2], ident[:])
             return turned
 
         def group(store, u, name, turned):
@@ -117,9 +132,9 @@ def tile_multiscaleretention_pb_t_kernel(tc, x_bytes, x_scale, y_norm, wg_w, wo_
 
         def turn(u):
             c, rows = rows_of(u)
-            x_words = x_scaled[u][:].bitcast(F32).rearrange("p (j w) -> p j w", j=PAIR)
+            x_words = [tokens.bitcast(F32) for tokens in x_scaled[u]]
             x_turned = transpose_pair(f"x_turned{u}", x_words)
-            y_words = y_raw[c][:, rows, :].rearrange("p j k -> p (j k)").bitcast(F32).rearrange("p (j w) -> p j w", j=PAIR)
+            y_words = [y_raw[c][:, j, :].bitcast(F32) for j in range(rows.start, rows.stop)]
             y_turned = transpose_pair(f"y_turned{u}", y_words)
             group(x_grouped, u, "x_grouped", x_turned)
             group(y_grouped, u, "y_grouped", y_turned)
@@ -151,7 +166,7 @@ def tile_multiscaleretention_pb_t_kernel(tc, x_bytes, x_scale, y_norm, wg_w, wo_
                     multiply(gates[u, j][:, t, :], (wg_codes, wg_scales), slice(t * P, (t + 1) * P), x_mx[u], slice(j * P, (j + 1) * P))
 
         def gated(u):
-            h_grouped[u] = work.tile([P, PAIR, P * PACK], BF16, name=f"h_grouped{u}", tag="h_grouped", align_bytes=64)
+            h_grouped[u] = h_ring[u % 3]
             for j in range(PAIR):
                 nc.vector.scalar_tensor_tensor(
                     out=h_grouped[u][:, j, :].rearrange("p (n t) -> p n t", t=PACK),
@@ -186,6 +201,8 @@ def tile_multiscaleretention_pb_t_kernel(tc, x_bytes, x_scale, y_norm, wg_w, wo_
                 load_y(s // UNITS_PER_CHUNK + 2, everything)
             if 0 <= s - 1:
                 output(s - 1)
+            if s + 4 < UNITS and helped(s + 4):
+                widen(s + 4)
             if 0 <= s < UNITS:
                 gated(s)
             if 0 <= s + 2 < UNITS:
@@ -200,6 +217,8 @@ def tile_multiscaleretention_pb_t_kernel(tc, x_bytes, x_scale, y_norm, wg_w, wo_
                 gate_matmuls(s + 1)
             if s + 3 < UNITS:
                 product(s + 3)
+                if helped(s + 3):
+                    product_gpsimd(s + 3)
             if s == -3:
                 nc.vector.tensor_copy(
                     out=wg_grouped[:].rearrange("p (t m j) -> p t m j", t=PACK, j=PACK),

@@ -13,6 +13,8 @@ CHUNKS = TOKENS // CHUNK
 PAIR = 2
 UNITS_PER_CHUNK = ROWS // PAIR
 UNITS = CHUNKS * UNITS_PER_CHUNK
+RING = 3
+HELP = 256
 
 FLOPS = 2 * 2 * TOKENS * DIM * DIM
 
@@ -78,8 +80,10 @@ def tile_multiscaleretention_pb_t_kernel(tc, x_bytes, x_scale, y_norm, wg_w, wo_
         nc.vector.tensor_copy(out=scale_row[:, 0, :].rearrange("p (n t) -> p n t", t=PACK), in_=spread_by_k)
         nc.scalar.copy(out=scale_row[:, 1, :].rearrange("p (n t) -> p n t", t=PACK), in_=spread_by_k)
 
-        h_ring = [keep.tile([P, PAIR, P * PACK], BF16, name=f"h_ring{i}", align_bytes=64) for i in range(3)]
+        ring = [keep.tile([P, PAIR, P * PACK], BF16, name=f"ring{i}", align_bytes=64) for i in range(RING)]
         x_wide = {}
+        turned = {}
+        accs = {}
         x_scaled = {}
         x_grouped = {}
         y_grouped = {}
@@ -93,51 +97,51 @@ def tile_multiscaleretention_pb_t_kernel(tc, x_bytes, x_scale, y_norm, wg_w, wo_
             return c, slice(i * PAIR, (i + 1) * PAIR)
 
         def helped(u):
-            return u >= 4 and u % 2 == 0
+            return u >= RING + 1
 
         def widen(u):
             c, rows = rows_of(u)
-            x_wide[u] = work.tile([P, DIM], BF16, name=f"x_wide{u}", tag="x_wide", align_bytes=64)
-            nc.scalar.copy(out=x_wide[u][:], in_=x_raw[c][:, rows.stop - 1, :].bitcast(FP8))
+            x_wide[u] = work.tile([P, HELP], BF16, name=f"x_wide{u}", tag="x_wide", align_bytes=64)
+            nc.scalar.copy(out=x_wide[u][:], in_=x_raw[c][:, rows.stop - 1, DIM - HELP :].bitcast(FP8))
 
         def product(u):
             c, rows = rows_of(u)
-            scaled = work.tile([P, PAIR * DIM], BF16, name=f"x_scaled{u}", tag="x_scaled", align_bytes=64)
+            x_scaled[u] = ring[(u - 1) % RING]
+            scaled = x_scaled[u][:].rearrange("p j k -> p (j k)")
             codes = x_raw[c][:, rows, :].rearrange("p j k -> p (j k)").bitcast(FP8)
             scales = scale_row[:].rearrange("p j k -> p (j k)")
-            pieces = PAIR if u == 0 or helped(u) else 1
-            width = PAIR * DIM // pieces
-            for i in range(1 if helped(u) else pieces):
-                cols = slice(i * width, (i + 1) * width)
+            own = PAIR * DIM - (HELP if helped(u) else 0)
+            pieces = [slice(0, DIM), slice(DIM, own)] if u == 0 else [slice(0, own)]
+            for cols in pieces:
                 nc.vector.tensor_tensor(out=scaled[:, cols], in0=codes[:, cols], in1=scales[:, cols], op=ALU.mult)
-            x_scaled[u] = [scaled[:, :DIM], scaled[:, DIM:]]
-
-        def product_gpsimd(u):
-            x_scaled[u][1] = h_ring[(u - 4) % 3][:, 0, :]
-            nc.gpsimd.tensor_tensor(out=x_scaled[u][1], in0=x_wide[u][:], in1=scale_row[:, 1, :], op=ALU.mult)
+            if helped(u):
+                nc.gpsimd.tensor_tensor(out=scaled[:, own:], in0=x_wide[u][:], in1=scales[:, own:], op=ALU.mult)
 
         def transpose_pair(name, words):
-            turned = psum.tile([P, PAIR, 2, P], F32, name=name, tag="words", bufs=4)
+            bank = psum.tile([P, PAIR, 2, P], F32, name=name, tag="words", bufs=4)
             for j in range(PAIR):
                 for half in range(2):
-                    nc.tensor.transpose(turned[:, j, half, :], words[j][:, half : DIM // 2 : 2], ident[:])
-            return turned
+                    nc.tensor.transpose(bank[:, j, half, :], words[j][:, half : DIM // 2 : 2], ident[:])
+            return bank
 
-        def group(store, u, name, turned):
+        def group(store, u, name, bank):
             store[u] = work.tile([P, PAIR, P * PACK], BF16, name=f"{name}{u}", tag=name, align_bytes=64)
             nc.scalar.copy(
                 out=store[u][:].rearrange("p j n -> p (j n)").bitcast(F32).rearrange("p (j n h) -> p j n h", j=PAIR, h=2),
-                in_=turned[:].rearrange("p j h n -> p j n h"),
+                in_=bank[:].rearrange("p j h n -> p j n h"),
             )
 
         def turn(u):
             c, rows = rows_of(u)
-            x_words = [tokens.bitcast(F32) for tokens in x_scaled[u]]
+            x_words = [x_scaled[u][:, j, :].bitcast(F32) for j in range(PAIR)]
             x_turned = transpose_pair(f"x_turned{u}", x_words)
             y_words = [y_raw[c][:, j, :].bitcast(F32) for j in range(rows.start, rows.stop)]
             y_turned = transpose_pair(f"y_turned{u}", y_words)
-            group(x_grouped, u, "x_grouped", x_turned)
-            group(y_grouped, u, "y_grouped", y_turned)
+            turned[u] = x_turned, y_turned
+
+        def group_unit(u):
+            group(x_grouped, u, "x_grouped", turned[u][0])
+            group(y_grouped, u, "y_grouped", turned[u][1])
 
         def quantize(codes, scales, grouped):
             nc.vector.quantize_mx(out=codes.bitcast(FP8X4), scales=scales, in_=grouped)
@@ -166,7 +170,7 @@ def tile_multiscaleretention_pb_t_kernel(tc, x_bytes, x_scale, y_norm, wg_w, wo_
                     multiply(gates[u, j][:, t, :], (wg_codes, wg_scales), slice(t * P, (t + 1) * P), x_mx[u], slice(j * P, (j + 1) * P))
 
         def gated(u):
-            h_grouped[u] = h_ring[u % 3]
+            h_grouped[u] = ring[u % RING]
             for j in range(PAIR):
                 nc.vector.scalar_tensor_tensor(
                     out=h_grouped[u][:, j, :].rearrange("p (n t) -> p n t", t=PACK),
@@ -177,36 +181,44 @@ def tile_multiscaleretention_pb_t_kernel(tc, x_bytes, x_scale, y_norm, wg_w, wo_
                     op1=ALU.mult,
                 )
 
+        def output_matmuls(u):
+            for j in range(PAIR):
+                accs[u, j] = psum.tile([P, DIM], F32, name=f"acc{u}_{j}", tag="acc", bufs=2)
+                multiply(accs[u, j][:], h_mx[u], slice(j * P, (j + 1) * P), (wo_codes, wo_scales), slice(0, DIM))
+
         def output(u):
             c, rows = rows_of(u)
             result = work.tile([P, PAIR, DIM], F32, name=f"result{u}", tag="result", bufs=4)
-            accs = []
-            for j in range(PAIR):
-                acc = psum.tile([P, DIM], F32, name=f"acc{u}_{j}", tag="acc", bufs=2)
-                multiply(acc[:], h_mx[u], slice(j * P, (j + 1) * P), (wo_codes, wo_scales), slice(0, DIM))
-                accs.append(acc)
-            if u < UNITS - 1:
+            if u < UNITS - 2:
                 for j in range(PAIR):
-                    nc.scalar.copy(out=result[:, j, :], in_=accs[j][:])
+                    nc.scalar.copy(out=result[:, j, :], in_=accs[u, j][:])
                 nc.sync.dma_start(out=out_hbm[c][:, rows, :], in_=result[:])
             else:
-                nc.scalar.copy(out=result[:, 0, :], in_=accs[0][:])
-                nc.vector.tensor_copy(out=result[:, 1, :], in_=accs[1][:])
+                nc.scalar.copy(out=result[:, 0, :], in_=accs[u, 0][:])
+                nc.vector.tensor_copy(out=result[:, 1, :], in_=accs[u, 1][:])
                 for j in range(PAIR):
                     nc.sync.dma_start(out=out_hbm[c][:, rows.start + j, :], in_=result[:, j, :])
 
-        for s in range(-3, UNITS + 1):
+        def group_wg(engine_copy, blocks):
+            engine_copy(
+                out=wg_grouped[:].rearrange("p (t m j) -> p t m j", t=PACK, j=PACK)[:, blocks],
+                in_=wg_raw[:].rearrange("p j (m t) -> p t m j", t=PACK)[:, blocks],
+            )
+
+        for s in range(-3, UNITS + 2):
             if s >= 0 and s % UNITS_PER_CHUNK == 0 and s // UNITS_PER_CHUNK + 2 < CHUNKS:
                 load_x(s // UNITS_PER_CHUNK + 2, everything)
                 load_y(s // UNITS_PER_CHUNK + 2, everything)
-            if 0 <= s - 1:
-                output(s - 1)
             if s + 4 < UNITS and helped(s + 4):
                 widen(s + 4)
             if 0 <= s < UNITS:
                 gated(s)
             if 0 <= s + 2 < UNITS:
                 turn(s + 2)
+            if 0 <= s - 2:
+                output(s - 2)
+            if 0 <= s + 2 < UNITS:
+                group_unit(s + 2)
             if s == -1:
                 nc.scalar.copy(
                     out=wo_grouped[:].rearrange("p (n j) -> p n j", j=PACK),
@@ -215,15 +227,13 @@ def tile_multiscaleretention_pb_t_kernel(tc, x_bytes, x_scale, y_norm, wg_w, wo_
             if 0 <= s + 1 < UNITS:
                 x_mx[s + 1] = quantize_unit("x", s + 1, x_grouped[s + 1])
                 gate_matmuls(s + 1)
+            if 0 <= s - 1 < UNITS:
+                output_matmuls(s - 1)
             if s + 3 < UNITS:
                 product(s + 3)
-                if helped(s + 3):
-                    product_gpsimd(s + 3)
             if s == -3:
-                nc.vector.tensor_copy(
-                    out=wg_grouped[:].rearrange("p (t m j) -> p t m j", t=PACK, j=PACK),
-                    in_=wg_raw[:].rearrange("p j (m t) -> p t m j", t=PACK),
-                )
+                group_wg(nc.scalar.copy, slice(0, 2))
+                group_wg(nc.vector.tensor_copy, slice(2, 4))
             if s == -2:
                 quantize(wg_codes[:], wg_scales[:], wg_grouped[:])
             if 0 <= s < UNITS:

@@ -14,7 +14,7 @@ PAIR = 2
 UNITS_PER_CHUNK = ROWS // PAIR
 UNITS = CHUNKS * UNITS_PER_CHUNK
 RING = 3
-HELP = 256
+HELP = 320
 
 FLOPS = 2 * 2 * TOKENS * DIM * DIM
 
@@ -183,13 +183,14 @@ def tile_multiscaleretention_pb_t_kernel(tc, x_bytes, x_scale, y_norm, wg_w, wo_
 
         def output_matmuls(u):
             for j in range(PAIR):
-                accs[u, j] = psum.tile([P, DIM], F32, name=f"acc{u}_{j}", tag="acc", bufs=2)
+                spare = u == UNITS - 3 or u == UNITS - 1
+                accs[u, j] = psum.tile([P, DIM], F32, name=f"acc{u}_{j}", tag="words" if spare else "acc", bufs=4 if spare else 2)
                 multiply(accs[u, j][:], h_mx[u], slice(j * P, (j + 1) * P), (wo_codes, wo_scales), slice(0, DIM))
 
         def output(u):
             c, rows = rows_of(u)
             result = work.tile([P, PAIR, DIM], F32, name=f"result{u}", tag="result", bufs=4)
-            if u < UNITS - 2:
+            if u < UNITS - 1:
                 for j in range(PAIR):
                     nc.scalar.copy(out=result[:, j, :], in_=accs[u, j][:])
                 nc.sync.dma_start(out=out_hbm[c][:, rows, :], in_=result[:])
@@ -211,12 +212,17 @@ def tile_multiscaleretention_pb_t_kernel(tc, x_bytes, x_scale, y_norm, wg_w, wo_
                 load_y(s // UNITS_PER_CHUNK + 2, everything)
             if s + 4 < UNITS and helped(s + 4):
                 widen(s + 4)
+            tail = s >= UNITS - 2
+            if 0 <= s + 1 < UNITS:
+                x_mx[s + 1] = quantize_unit("x", s + 1, x_grouped[s + 1])
             if 0 <= s < UNITS:
                 gated(s)
             if 0 <= s + 2 < UNITS:
                 turn(s + 2)
             if 0 <= s - 2:
                 output(s - 2)
+            if tail and s - 1 < UNITS:
+                output_matmuls(s - 1)
             if 0 <= s + 2 < UNITS:
                 group_unit(s + 2)
             if s == -1:
@@ -225,9 +231,8 @@ def tile_multiscaleretention_pb_t_kernel(tc, x_bytes, x_scale, y_norm, wg_w, wo_
                     in_=wo_raw[:].rearrange("p j n -> p n j"),
                 )
             if 0 <= s + 1 < UNITS:
-                x_mx[s + 1] = quantize_unit("x", s + 1, x_grouped[s + 1])
                 gate_matmuls(s + 1)
-            if 0 <= s - 1 < UNITS:
+            if not tail and 0 <= s - 1:
                 output_matmuls(s - 1)
             if s + 3 < UNITS:
                 product(s + 3)

from contextlib import ExitStack

import concourse.mybir as mybir
from concourse.masks import make_identity

P = 128
PACK = 4
DIM = 512
TOKENS = 4 * 2048
ROWS = 8
CHUNK = P * ROWS
CHUNKS = TOKENS // CHUNK
PAIR = 2
UNITS_PER_CHUNK = ROWS // PAIR
UNITS = CHUNKS * UNITS_PER_CHUNK
RING = 3
HELP = 320

FLOPS = 2 * 2 * TOKENS * DIM * DIM

F32 = mybir.dt.float32
BF16 = mybir.dt.bfloat16
U32 = mybir.dt.uint32
U8 = mybir.dt.uint8
FP8 = mybir.dt.float8_e4m3fn
FP8X4 = mybir.dt.float8_e4m3fn_x4
ALU = mybir.AluOpType


def tile_multiscaleretention_pb_t_kernel(tc, x_bytes, x_scale, y_norm, wg_w, wo_w, out):
    nc = tc.nc
    x_hbm = x_bytes.rearrange("b s k -> (b s) k").rearrange("(c p j) k -> c p j k", p=P, j=ROWS)
    y_hbm = y_norm.rearrange("b s k -> (b s) k").rearrange("(c p j) k -> c p j k", p=P, j=ROWS)
    out_hbm = out.rearrange("b s k -> (b s) k").rearrange("(c p j) k -> c p j k", p=P, j=ROWS)

    with ExitStack() as ctx:
        keep = ctx.enter_context(tc.tile_pool(name="keep", bufs=1))
        work = ctx.enter_context(tc.tile_pool(name="work", bufs=3))
        psum = ctx.enter_context(tc.psum_pool(name="psum", bufs=2))
        ctx.enter_context(tc.manual_schedule())

        x_raw = [keep.tile([P, ROWS, DIM], U8, name=f"x_raw{c}", align_bytes=64) for c in range(CHUNKS)]
        y_raw = [keep.tile([P, ROWS, DIM], BF16, name=f"y_raw{c}", align_bytes=64) for c in range(CHUNKS)]
        scale_col = keep.tile([P, PACK], F32, name="scale_col")
        scale_row = keep.tile([P, PAIR, DIM], F32, name="scale_row", align_bytes=64)
        ident = keep.tile([P, P], F32, name="ident")
        wg_raw = keep.tile([P, PACK, DIM], BF16, name="wg_raw", align_bytes=64)
        wo_raw = keep.tile([P, PACK, DIM], BF16, name="wo_raw", align_bytes=64)
        wg_grouped = keep.tile([P, DIM * PACK], BF16, name="wg_grouped", align_bytes=64)
        wo_grouped = keep.tile([P, DIM * PACK], BF16, name="wo_grouped", align_bytes=64)
        wg_codes = keep.tile([P, DIM], U32, name="wg_codes", align_bytes=64)
        wo_codes = keep.tile([P, DIM], U32, name="wo_codes", align_bytes=64)
        wg_scales = keep.tile([P, DIM], U8, name="wg_scales", align_bytes=64)
        wo_scales = keep.tile([P, DIM], U8, name="wo_scales", align_bytes=64)

        def load_x(c, rows):
            nc.sync.dma_start(out=x_raw[c][:, rows, :], in_=x_hbm[c][:, rows, :])

        def load_y(c, rows):
            nc.sync.dma_start(out=y_raw[c][:, rows, :], in_=y_hbm[c][:, rows, :])

        everything = slice(0, ROWS)
        first = slice(0, PAIR)
        rest = slice(PAIR, ROWS)
        nc.sync.dma_start(out=scale_col[:], in_=x_scale.rearrange("a b (p t) -> p (a b t)", t=PACK))
        load_x(0, first)
        nc.sync.dma_start(out=wg_raw[:], in_=wg_w.rearrange("(p j) n -> p j n", j=PACK))
        load_x(0, rest)
        load_y(0, first)
        nc.sync.dma_start(out=wo_raw[:], in_=wo_w.rearrange("(p j) n -> p j n", j=PACK))
        load_y(0, rest)
        load_x(1, everything)
        load_y(1, everything)

        make_identity(nc, ident[:])
        spread = psum.tile([P, PACK, P], F32, name="spread", tag="words", bufs=4)
        for t in range(PACK):
            nc.tensor.transpose(spread[:, t, :], scale_col[:, t : t + 1].to_broadcast([P, P]), ident[:])
        spread_by_k = spread[:].rearrange("p t n -> p n t")
        nc.vector.tensor_copy(out=scale_row[:, 0, :].rearrange("p (n t) -> p n t", t=PACK), in_=spread_by_k)
        nc.scalar.copy(out=scale_row[:, 1, :].rearrange("p (n t) -> p n t", t=PACK), in_=spread_by_k)

        ring = [keep.tile([P, PAIR, P * PACK], BF16, name=f"ring{i}", align_bytes=64) for i in range(RING)]
        x_wide = {}
        turned = {}
        accs = {}
        x_scaled = {}
        x_grouped = {}
        y_grouped = {}
        x_mx = {}
        gates = {}
        h_grouped = {}
        h_mx = {}

        def rows_of(u):
            c, i = divmod(u, UNITS_PER_CHUNK)
            return c, slice(i * PAIR, (i + 1) * PAIR)

        def helped(u):
            return u >= RING + 1

        def widen(u):
            c, rows = rows_of(u)
            x_wide[u] = work.tile([P, HELP], BF16, name=f"x_wide{u}", tag="x_wide", align_bytes=64)
            nc.scalar.copy(out=x_wide[u][:], in_=x_raw[c][:, rows.stop - 1, DIM - HELP :].bitcast(FP8))

        def product(u):
            c, rows = rows_of(u)
            x_scaled[u] = ring[(u - 1) % RING]
            scaled = x_scaled[u][:].rearrange("p j k -> p (j k)")
            codes = x_raw[c][:, rows, :].rearrange("p j k -> p (j k)").bitcast(FP8)
            scales = scale_row[:].rearrange("p j k -> p (j k)")
            own = PAIR * DIM - (HELP if helped(u) else 0)
            pieces = [slice(0, DIM), slice(DIM, own)] if u == 0 else [slice(0, own)]
            for cols in pieces:
                nc.vector.tensor_tensor(out=scaled[:, cols], in0=codes[:, cols], in1=scales[:, cols], op=ALU.mult)
            if helped(u):
                nc.gpsimd.tensor_tensor(out=scaled[:, own:], in0=x_wide[u][:], in1=scales[:, own:], op=ALU.mult)

        def transpose_pair(name, words):
            bank = psum.tile([P, PAIR, 2, P], F32, name=name, tag="words", bufs=4)
            for j in range(PAIR):
                for half in range(2):
                    nc.tensor.transpose(bank[:, j, half, :], words[j][:, half : DIM // 2 : 2], ident[:])
            return bank

        def group(store, u, name, bank):
            store[u] = work.tile([P, PAIR, P * PACK], BF16, name=f"{name}{u}", tag=name, align_bytes=64)
            nc.scalar.copy(
                out=store[u][:].rearrange("p j n -> p (j n)").bitcast(F32).rearrange("p (j n h) -> p j n h", j=PAIR, h=2),
                in_=bank[:].rearrange("p j h n -> p j n h"),
            )

        def turn(u):
            c, rows = rows_of(u)
            x_words = [x_scaled[u][:, j, :].bitcast(F32) for j in range(PAIR)]
            x_turned = transpose_pair(f"x_turned{u}", x_words)
            y_words = [y_raw[c][:, j, :].bitcast(F32) for j in range(rows.start, rows.stop)]
            y_turned = transpose_pair(f"y_turned{u}", y_words)
            turned[u] = x_turned, y_turned

        def group_unit(u):
            group(x_grouped, u, "x_grouped", turned[u][0])
            group(y_grouped, u, "y_grouped", turned[u][1])

        def quantize(codes, scales, grouped):
            nc.vector.quantize_mx(out=codes.bitcast(FP8X4), scales=scales, in_=grouped)

        def quantize_unit(name, u, grouped):
            codes = work.tile([P, PAIR * P], U32, name=f"{name}_codes{u}", tag=f"{name}_codes", align_bytes=64)
            scales = work.tile([P, PAIR * P], U8, name=f"{name}_scales{u}", tag=f"{name}_scales", align_bytes=64)
            quantize(codes[:], scales[:], grouped[:].rearrange("p j n -> p (j n)"))
            return codes, scales

        def multiply(dst, left, left_cols, right, right_cols):
            nc.tensor.matmul_mx(
                out=dst,
                lhsT=left[0][:, left_cols].bitcast(FP8X4),
                lhsT_scale=left[1][:, left_cols],
                rhs=right[0][:, right_cols].bitcast(FP8X4),
                rhs_scale=right[1][:, right_cols],
                start=True,
                stop=True,
            )

        def gate_matmuls(u):
            for j in range(PAIR):
                gates[u, j] = psum.tile([P, PACK, P], F32, name=f"gate{u}_{j}", tag="gate", bufs=2)
                for t in range(PACK):
                    multiply(gates[u, j][:, t, :], (wg_codes, wg_scales), slice(t * P, (t + 1) * P), x_mx[u], slice(j * P, (j + 1) * P))

        def gated(u):
            h_grouped[u] = ring[u % RING]
            for j in range(PAIR):
                nc.vector.scalar_tensor_tensor(
                    out=h_grouped[u][:, j, :].rearrange("p (n t) -> p n t", t=PACK),
                    in0=gates[u, j][:].rearrange("p t n -> p n t"),
                    scalar=0.0,
                    in1=y_grouped[u][:, j, :].rearrange("p (n t) -> p n t", t=PACK),
                    op0=ALU.max,
                    op1=ALU.mult,
                )

        def output_matmuls(u):
            for j in range(PAIR):
                spare = u == UNITS - 3 or u == UNITS - 1
                accs[u, j] = psum.tile([P, DIM], F32, name=f"acc{u}_{j}", tag="words" if spare else "acc", bufs=4 if spare else 2)
                multiply(accs[u, j][:], h_mx[u], slice(j * P, (j + 1) * P), (wo_codes, wo_scales), slice(0, DIM))

        def output(u):
            c, rows = rows_of(u)
            result = work.tile([P, PAIR, DIM], F32, name=f"result{u}", tag="result", bufs=4)
            if u < UNITS - 1:
                for j in range(PAIR):
                    nc.scalar.copy(out=result[:, j, :], in_=accs[u, j][:])
                nc.sync.dma_start(out=out_hbm[c][:, rows, :], in_=result[:])
            else:
                nc.scalar.copy(out=result[:, 0, :], in_=accs[u, 0][:])
                nc.vector.tensor_copy(out=result[:, 1, :], in_=accs[u, 1][:])
                for j in range(PAIR):
                    nc.sync.dma_start(out=out_hbm[c][:, rows.start + j, :], in_=result[:, j, :])

        def group_wg(engine_copy, blocks):
            engine_copy(
                out=wg_grouped[:].rearrange("p (t m j) -> p t m j", t=PACK, j=PACK)[:, blocks],
                in_=wg_raw[:].rearrange("p j (m t) -> p t m j", t=PACK)[:, blocks],
            )

        for s in range(-3, UNITS + 2):
            if s >= 0 and s % UNITS_PER_CHUNK == 0 and s // UNITS_PER_CHUNK + 2 < CHUNKS:
                load_x(s // UNITS_PER_CHUNK + 2, everything)
                load_y(s // UNITS_PER_CHUNK + 2, everything)
            if s + 4 < UNITS and helped(s + 4):
                widen(s + 4)
            tail = s >= UNITS - 2
            if 0 <= s + 1 < UNITS:
                x_mx[s + 1] = quantize_unit("x", s + 1, x_grouped[s + 1])
            if 0 <= s < UNITS:
                gated(s)
            if 0 <= s + 2 < UNITS:
                turn(s + 2)
            if 0 <= s - 2:
                output(s - 2)
            if tail and s - 1 < UNITS:
                output_matmuls(s - 1)
            if 0 <= s + 2 < UNITS:
                group_unit(s + 2)
            if s == -1:
                nc.scalar.copy(
                    out=wo_grouped[:].rearrange("p (n j) -> p n j", j=PACK),
                    in_=wo_raw[:].rearrange("p j n -> p n j"),
                )
            if 0 <= s + 1 < UNITS:
                gate_matmuls(s + 1)
            if not tail and 0 <= s - 1:
                output_matmuls(s - 1)
            if s + 3 < UNITS:
                product(s + 3)
            if s == -3:
                group_wg(nc.scalar.copy, slice(0, 2))
                group_wg(nc.vector.tensor_copy, slice(2, 4))
            if s == -2:
                quantize(wg_codes[:], wg_scales[:], wg_grouped[:])
            if 0 <= s < UNITS:
                h_mx[s] = quantize_unit("h", s, h_grouped[s])
            if s == 0:
                quantize(wo_codes[:], wo_scales[:], wo_grouped[:])
